import numpy as np
import ml_dtypes


def mxq(x, axis, fmt="e4m3"):
    dtype, down = {"e4m3": (ml_dtypes.float8_e4m3fn, 7), "e5m2": (ml_dtypes.float8_e5m2, 14)}[fmt]
    v = np.moveaxis(np.asarray(x, np.float32).astype(ml_dtypes.bfloat16).astype(np.float64), axis, -1)
    blocks = v.reshape(v.shape[:-1] + (-1, 32))
    amax = np.abs(blocks).max(-1, keepdims=True)
    byte = np.maximum(np.where(amax > 0, np.frexp(amax)[1] - 1 + 127, 0) - down, 1)
    scale = np.exp2(byte - 127.0)
    codes = (blocks / scale).astype(np.float32).astype(dtype).astype(np.float64)
    return np.moveaxis((codes * scale).reshape(v.shape), -1, axis)


WIDE = False


def mx_kscale(k):
    if not WIDE:
        return np.ones(k)
    levels = np.array([10, -10, 5, -5, 0])
    if k % 512:
        return np.exp2(np.random.permutation(np.resize(levels, k // 32))).repeat(32)
    a = np.empty((k // 512, 16))
    for p in range(k // 512):
        a[p, :8] = np.random.permutation(np.resize(levels, 8))
        for g in range(8):
            far = levels[np.abs(levels - a[p, g]) >= 10]
            a[p, g + 8] = far[np.random.randint(len(far))]
    return np.exp2(a.ravel()).repeat(32)


BF16 = ml_dtypes.bfloat16


def bf(x):
    return np.asarray(x, np.float32).astype(BF16)


def f64(x):
    return np.asarray(x).astype(np.float64)


B, T, C, CO, HS, DW, DA, DV, DG = 4, 1024, 1024, 256, 64, 128, 128, 128, 256
H = CO // HS
EPS_NORM = 1e-12


def sigmoid(u):
    return 1.0 / (1.0 + np.exp(-u))


def setup_inputs():
    n = np.random.standard_normal
    s = mx_kscale(C)
    return {
        "x": bf(n((B, T, C)) * s),
        "x_k": bf(n((1, 1, C)) * 0.3),
        "W_k": bf(n((CO, C)) / np.sqrt(C) / s),
        "a_hid": bf(n((B, T, DA))),
        "a2": bf(n((DA, CO)) / np.sqrt(DA)),
        "a0": bf(n((1, 1, CO)) * 0.5),
        "k_k": bf(0.71 + n((1, 1, CO)) * 0.2),
        "k_a": bf(1.02 + n((1, 1, CO)) * 0.2),
    }


def reference(x, x_k, W_k, a_hid, a2, a0, k_k, k_a):
    x = f64(x)
    prev = np.concatenate([np.zeros_like(x[:, :1]), x[:, :-1]], axis=1)
    xk = x + (prev - x) * f64(x_k)
    k = mxq(xk, 2, "e4m3") @ mxq(f64(W_k), 1, "e4m3").T
    a = sigmoid(f64(a0) + f64(a_hid) @ f64(a2))
    kkh = (k * f64(k_k)).reshape(B, T, H, HS)
    nrm = np.sqrt(np.sum(kkh * kkh, axis=-1, keepdims=True))
    kk = (kkh / np.maximum(nrm, EPS_NORM)).reshape(B, T, CO)
    k_out = k * (1.0 + (a - 1.0) * f64(k_a))
    return k_out, kk

@@ -1,0 +1,343 @@
+from contextlib import ExitStack
+
+import concourse.mybir as mybir
+from concourse.masks import make_identity
+
+F32 = mybir.dt.float32
+BF16 = mybir.dt.bfloat16
+U32 = mybir.dt.uint32
+U8 = mybir.dt.uint8
+FP8X4 = mybir.dt.float8_e4m3fn_x4
+ALU = mybir.AluOpType
+ACT = mybir.ActivationFunctionType
+
+P = 128
+PACK = 4
+B, T, C, CO, HS, DA = 4, 1024, 1024, 256, 64, 128
+PASSES = C // (P * PACK)
+CHUNKS = C // P
+CO_HALVES = CO // P
+UNIT = 512
+UNITS = B * T // UNIT
+UNITS_T = T // UNIT
+TILES_U = UNIT // P
+TILES = B * T // P
+STEPS_U = CHUNKS // 2
+STEPS = UNITS * STEPS_U
+GROUPS = UNITS * PASSES
+PAIRS = TILES // 2
+PAIRS_U = TILES_U // 2
+HEADS2 = 2 * CO // HS
+TILES_Q = 8
+QUARTERS = TILES // TILES_Q
+EPS_NORM = 1e-12
+
+FLOPS = 2 * B * T * C * CO + 2 * B * T * DA * CO
+
+
+def tile_full_tmix_params_pa_t_kernel(tc, x, x_k, W_k, a_hid, a2, a0, k_k, k_a, out_0, out_1):
+    nc = tc.nc
+    x_units = x.flatten_outer_dims().rearrange("(v n p) k -> v p n k", n=TILES_U, p=P)
+    a_rows = a_hid.flatten_outer_dims().rearrange("(n p) k -> p n k", p=P)
+    k_out_v = out_0.flatten_outer_dims().rearrange("(n p) c -> p n c", p=P)
+    kk_v = out_1.flatten_outer_dims().rearrange("(n p) c -> p n c", p=P)
+
+    with ExitStack() as ctx:
+        keep = ctx.enter_context(tc.tile_pool(name="keep", bufs=1))
+        work = ctx.enter_context(tc.tile_pool(name="work", bufs=2))
+        mx = ctx.enter_context(tc.tile_pool(name="mx", bufs=4))
+        tail = ctx.enter_context(tc.tile_pool(name="tail", bufs=3))
+        psum_t = ctx.enter_context(tc.psum_pool(name="psum_t", bufs=4))
+        psum_acc = ctx.enter_context(tc.psum_pool(name="psum_acc", bufs=4))
+
+        rows = keep.tile([P, P * PACK], BF16)
+        nc.vector.memset(rows[:], 0.0)
+        nc.sync.dma_start(out=rows[0:PASSES, :], in_=x_k.rearrange("a b (g c) -> (a b g) c", g=PASSES))
+        nc.sync.dma_start(out=rows[PASSES : PASSES + 1, 0:CO], in_=a0.rearrange("a b c -> (a b) c"))
+        w_sb = keep.tile([P, CO_HALVES, C], BF16)
+        nc.sync.dma_start(out=w_sb[:], in_=W_k.rearrange("(h p) k -> p h k", p=P))
+        a2_sb = keep.tile([P, CO], BF16)
+        a_sb = keep.tile([P, TILES, DA], BF16)
+        x_sb = []
+        for v in range(UNITS):
+            x_v = keep.tile([P, TILES_U, C], BF16, name="x_sb%d" % v)
+            nc.sync.dma_start(out=x_v[:], in_=x_units[v])
+            x_sb.append(x_v)
+            if v == 0:
+                nc.sync.dma_start(out=a2_sb[:], in_=a2)
+            if v < QUARTERS:
+                tiles_q = slice(TILES_Q * v, TILES_Q * (v + 1))
+                nc.sync.dma_start(out=a_sb[:, tiles_q, :], in_=a_rows[:, tiles_q, :])
+        ka_b = keep.tile([P, CO], BF16)
+        nc.scalar.dma_start(out=ka_b[:], in_=k_a.rearrange("a b c -> (a b c)").partition_broadcast(P))
+        kk_b = keep.tile([P, CO], BF16)
+        nc.scalar.dma_start(out=kk_b[:], in_=k_k.rearrange("a b c -> (a b c)").partition_broadcast(P))
+
+        ident = keep.tile([P, P], BF16)
+        make_identity(nc, ident[:])
+        ident_f32 = keep.tile([P, P], F32)
+        make_identity(nc, ident_f32[:])
+
+        u = []
+        for chunk in range(CHUNKS):
+            u_c = keep.tile([P, T + 1], F32, name="u%d" % chunk)
+            nc.vector.memset(u_c[:, 0:1], 0.0)
+            u.append(u_c)
+        eps2 = keep.tile([P, 1], F32)
+        nc.vector.memset(eps2[:], EPS_NORM * EPS_NORM)
+        neg_eps2 = keep.tile([P, 1], F32)
+        nc.vector.memset(neg_eps2[:], -EPS_NORM * EPS_NORM)
+
+        rows_ps = psum_t.tile([P, PACK + CO_HALVES, P], BF16, tag="t")
+        for j in range(PACK):
+            nc.tensor.transpose(out=rows_ps[:, j, :], in_=rows[:, j : P * PACK : PACK], identity=ident[:])
+        for h in range(CO_HALVES):
+            nc.tensor.transpose(out=rows_ps[:, PACK + h, :], in_=rows[:, h * P : (h + 1) * P], identity=ident[:])
+        mix = keep.tile([P, CHUNKS], F32)
+        nc.vector.tensor_copy(
+            out=mix[:].rearrange("p (g j) -> p g j", g=PASSES),
+            in_=rows_ps[:, 0:PACK, 0:PASSES].rearrange("p j g -> p g j"),
+        )
+        stay = keep.tile([P, CHUNKS], F32)
+        nc.vector.tensor_scalar(out=stay[:], in0=mix[:], scalar1=-1.0, scalar2=1.0, op0=ALU.mult, op1=ALU.add)
+        a0_cols = keep.tile([P, CO_HALVES, P], F32)
+        for h in range(CO_HALVES):
+            nc.vector.tensor_copy(
+                out=a0_cols[:, h, :], in_=rows_ps[:, PACK + h, PASSES : PASSES + 1].to_broadcast([P, P])
+            )
+
+        w_codes = keep.tile([P, PASSES, CO], U32, align_bytes=64)
+        w_scales = keep.tile([P, PASSES, CO], U8, align_bytes=64)
+        for g in range(PASSES):
+            wT_ps = psum_acc.tile([P, PACK, CO], BF16, tag="acc")
+            for j in range(PACK):
+                for h in range(CO_HALVES):
+                    nc.tensor.transpose(
+                        out=wT_ps[:, j, h * P : (h + 1) * P],
+                        in_=w_sb[:, h, g * P * PACK + j : (g + 1) * P * PACK : PACK],
+                        identity=ident[:],
+                    )
+            w_grouped = work.tile([P, CO, PACK], BF16, align_bytes=64)
+            nc.vector.tensor_copy(out=w_grouped[:], in_=wT_ps[:].rearrange("p j c -> p c j"))
+            nc.vector.quantize_mx(
+                out=w_codes[:, g, :].bitcast(FP8X4),
+                scales=w_scales[:, g, :],
+                in_=w_grouped[:].rearrange("p c j -> p (c j)"),
+            )
+
+        ahT = keep.tile([P, TILES, P], BF16)
+        gate1 = keep.tile([P, TILES, CO], F32)
+
+        def transpose_a_hid(q):
+            ahT_ps = psum_acc.tile([P, TILES_Q, P], BF16, tag="acc")
+            for n in range(TILES_Q):
+                nc.tensor.transpose(out=ahT_ps[:, n, :], in_=a_sb[:, TILES_Q * q + n, :], identity=ident[:])
+            nc.scalar.copy(out=ahT[:, TILES_Q * q : TILES_Q * (q + 1), :], in_=ahT_ps[:])
+
+        def gate(pair):
+            z_ps = psum_acc.tile([P, 2, CO], F32, tag="acc")
+            for e in range(2):
+                for h in range(CO_HALVES):
+                    nc.tensor.matmul(
+                        out=z_ps[:, e, h * P : (h + 1) * P],
+                        lhsT=a0_cols[:, h, :],
+                        rhs=ident_f32[:],
+                        is_transpose=True,
+                        start=(h == 0),
+                        stop=False,
+                    )
+                nc.tensor.matmul(out=z_ps[:, e, :], lhsT=ahT[:, 2 * pair + e, :], rhs=a2_sb[:], start=False, stop=True)
+            a_gate = tail.tile([P, 2, CO], F32)
+            nc.scalar.activation(out=a_gate[:], in_=z_ps[:], func=ACT.Sigmoid)
+            nc.vector.scalar_tensor_tensor(
+                out=gate1[:, 2 * pair : 2 * pair + 2, :],
+                in0=a_gate[:],
+                scalar=1.0,
+                in1=ka_b[:].unsqueeze(1).to_broadcast([P, 2, CO]),
+                op0=ALU.subtract,
+                op1=ALU.mult,
+            )
+
+        def gate_quarter(q):
+            for pair in range(TILES_Q // 2 * q, TILES_Q // 2 * (q + 1)):
+                gate(pair)
+
+        xT = {}
+        planes = {}
+        grouped = {}
+        codes = {}
+        scales = {}
+        k_ps = {}
+        kkh = {}
+        sumsq = {}
+        floored = {}
+        inv_norm = {}
+
+        def transpose_x(s):
+            v, pos = divmod(s, STEPS_U)
+            bank = psum_t.tile([P, 2, UNIT], BF16, tag="t")
+            for cc in range(2):
+                g, j = divmod(2 * pos + cc, PACK)
+                for n in range(TILES_U):
+                    nc.tensor.transpose(
+                        out=bank[:, cc, n * P : (n + 1) * P],
+                        in_=x_sb[v][:, n, g * P * PACK + j : (g + 1) * P * PACK : PACK],
+                        identity=ident[:],
+                    )
+            xT[s] = bank
+
+        def scale_prev(s):
+            v, pos = divmod(s, STEPS_U)
+            first = UNIT * (v % UNITS_T)
+            for cc in range(2):
+                chunk = 2 * pos + cc
+                nc.scalar.activation(
+                    out=u[chunk][:, first + 1 : first + 1 + UNIT],
+                    in_=xT[s][:, cc, :],
+                    func=ACT.Copy,
+                    scale=mix[:, chunk : chunk + 1],
+                )
+
+        def mix_tokens(s):
+            v, pos = divmod(s, STEPS_U)
+            first = UNIT * (v % UNITS_T)
+            i = s // 2
+            if s % 2 == 0:
+                new_planes = work.tile([P, PACK, UNIT], BF16, tag="planes")
+                planes[i] = new_planes
+            for cc in range(2):
+                chunk = 2 * pos + cc
+                nc.vector.scalar_tensor_tensor(
+                    out=planes[i][:, chunk % PACK, :],
+                    in0=xT[s][:, cc, :],
+                    scalar=stay[:, chunk : chunk + 1],
+                    in1=u[chunk][:, first : first + UNIT],
+                    op0=ALU.mult,
+                    op1=ALU.add,
+                )
+
+        def step(s):
+            if s + 3 < STEPS:
+                transpose_x(s + 3)
+            if s + 2 < STEPS:
+                scale_prev(s + 2)
+            if s < STEPS:
+                mix_tokens(s)
+
+        def regroup(i):
+            new_grouped = keep.tile([P, UNIT, PACK], BF16, align_bytes=64, tag="grouped")
+            nc.gpsimd.tensor_scalar(
+                out=new_grouped[:],
+                in0=planes[i][:].rearrange("p j r -> p r j"),
+                scalar1=1.0,
+                scalar2=0.0,
+                op0=ALU.mult,
+                op1=ALU.add,
+            )
+            grouped[i] = new_grouped
+
+        def quantise(i):
+            new_codes = mx.tile([P, UNIT], U32, align_bytes=64, tag="codes")
+            new_scales = mx.tile([P, UNIT], U8, align_bytes=64, tag="scales")
+            nc.vector.quantize_mx(
+                out=new_codes[:].bitcast(FP8X4),
+                scales=new_scales[:],
+                in_=grouped[i][:].rearrange("p r j -> p (r j)"),
+            )
+            codes[i] = new_codes
+            scales[i] = new_scales
+
+        def project(pair):
+            v, pos = divmod(pair, PAIRS_U)
+            acc = psum_acc.tile([P, 2, CO], F32, tag="acc")
+            for e in range(2):
+                tokens = slice((2 * pos + e) * P, (2 * pos + e + 1) * P)
+                for g in range(PASSES):
+                    nc.tensor.matmul_mx(
+                        out=acc[:, e, :],
+                        lhsT=codes[PASSES * v + g][:, tokens].bitcast(FP8X4),
+                        lhsT_scale=scales[PASSES * v + g][:, tokens],
+                        rhs=w_codes[:, g, :].bitcast(FP8X4),
+                        rhs_scale=w_scales[:, g, :],
+                        start=(g == 0),
+                        stop=(g == PASSES - 1),
+                    )
+            k_ps[pair] = acc
+
+        def scale_k(pair):
+            new_kkh = tail.tile([P, HEADS2, HS], F32, tag="kkh")
+            nc.vector.tensor_tensor(
+                out=new_kkh[:].rearrange("p (e h) d -> p e (h d)", e=2),
+                in0=k_ps[pair][:],
+                in1=kk_b[:].unsqueeze(1).to_broadcast([P, 2, CO]),
+                op=ALU.mult,
+            )
+            kkh[pair] = new_kkh
+            k_out_sb = tail.tile([P, 2, CO], F32)
+            nc.vector.scalar_tensor_tensor(
+                out=k_out_sb[:],
+                in0=gate1[:, 2 * pair : 2 * pair + 2, :],
+                scalar=1.0,
+                in1=k_ps[pair][:],
+                op0=ALU.add,
+                op1=ALU.mult,
+            )
+            nc.sync.dma_start(out=k_out_v[:, 2 * pair : 2 * pair + 2, :], in_=k_out_sb[:])
+
+        def sum_squares(pair):
+            squares = tail.tile([P, HEADS2, HS], F32)
+            new_sumsq = tail.tile([P, HEADS2], F32, tag="sumsq")
+            for h in range(HEADS2):
+                nc.scalar.activation(
+                    out=squares[:, h, :], in_=kkh[pair][:, h, :], func=ACT.Square, accum_out=new_sumsq[:, h : h + 1]
+                )
+            sumsq[pair] = new_sumsq
+
+        def floor_sum(pair):
+            new_floored = tail.tile([P, HEADS2], F32, tag="floored")
+            nc.scalar.activation(out=new_floored[:], in_=sumsq[pair][:], func=ACT.Relu, bias=neg_eps2[:])
+            floored[pair] = new_floored
+
+        def invert_norm(pair):
+            new_inv = tail.tile([P, HEADS2], F32, tag="inv_norm")
+            nc.scalar.activation(out=new_inv[:], in_=floored[pair][:], func=ACT.Abs_reciprocal_sqrt, bias=eps2[:])
+            inv_norm[pair] = new_inv
+
+        def divide(pair):
+            kk_sb = tail.tile([P, HEADS2, HS], F32)
+            for h in range(HEADS2):
+                nc.scalar.activation(
+                    out=kk_sb[:, h, :], in_=kkh[pair][:, h, :], func=ACT.Copy, scale=inv_norm[pair][:, h : h + 1]
+                )
+            nc.sync.dma_start(
+                out=kk_v[:, 2 * pair : 2 * pair + 2, :], in_=kk_sb[:].rearrange("p (e h) d -> p e (h d)", e=2)
+            )
+
+        for s in range(3):
+            transpose_x(s)
+        for s in range(2):
+            scale_prev(s)
+        transpose_a_hid(0)
+        for i in range(GROUPS + 5):
+            if 0 <= i - 4 < PAIRS:
+                sum_squares(i - 4)
+            step(2 * i)
+            if 0 <= i - 4 < PAIRS:
+                floor_sum(i - 4)
+            if 0 <= i - 5 < PAIRS:
+                divide(i - 5)
+            if 0 <= i - 4 < PAIRS:
+                invert_norm(i - 4)
+            step(2 * i + 1)
+            if 0 <= i - 1 < GROUPS:
+                quantise(i - 1)
+            if i < GROUPS:
+                regroup(i)
+            if 0 <= i - 3 < PAIRS:
+                scale_k(i - 3)
+            if i < QUARTERS:
+                gate_quarter(i)
+            if i + 1 < QUARTERS:
+                transpose_a_hid(i + 1)
+            if 0 <= i - 2 < PAIRS:
+                project(i - 2)

@@ -17,6 +17,8 @@ B, T, C, CO, HS, DA = 4, 1024, 1024, 256, 64, 128
 PASSES = C // (P * PACK)
 CHUNKS = C // P
 CO_HALVES = CO // P
+DUOS = PACK // 2
+A0_ROW, KK_ROW, KA_ROW = PASSES, PASSES + 1, PASSES + 2
 UNIT = 512
 UNITS = B * T // UNIT
 UNITS_T = T // UNIT
@@ -51,27 +53,34 @@ def tile_full_tmix_params_pa_t_kernel(tc, x, x_k, W_k, a_hid, a2, a0, k_k, k_a, 
         psum_acc = ctx.enter_context(tc.psum_pool(name="psum_acc", bufs=4))
 
         rows = keep.tile([P, P * PACK], BF16)
-        nc.vector.memset(rows[:], 0.0)
+        nc.gpsimd.memset(rows[:], 0.0)
         nc.sync.dma_start(out=rows[0:PASSES, :], in_=x_k.rearrange("a b (g c) -> (a b g) c", g=PASSES))
-        nc.sync.dma_start(out=rows[PASSES : PASSES + 1, 0:CO], in_=a0.rearrange("a b c -> (a b) c"))
+        for r, vector in ((A0_ROW, a0), (KK_ROW, k_k), (KA_ROW, k_a)):
+            nc.sync.dma_start(out=rows[r : r + 1, 0:CO], in_=vector.rearrange("a b c -> (a b) c"))
         w_sb = keep.tile([P, CO_HALVES, C], BF16)
-        nc.sync.dma_start(out=w_sb[:], in_=W_k.rearrange("(h p) k -> p h k", p=P))
         a2_sb = keep.tile([P, CO], BF16)
         a_sb = keep.tile([P, TILES, DA], BF16)
         x_sb = []
         for v in range(UNITS):
             x_v = keep.tile([P, TILES_U, C], BF16, name="x_sb%d" % v)
-            nc.sync.dma_start(out=x_v[:], in_=x_units[v])
+            if v == 0:
+                for g in range(PASSES):
+                    channels = slice(g * P * PACK, (g + 1) * P * PACK)
+                    nc.sync.dma_start(out=x_v[:, :, channels], in_=x_units[v][:, :, channels])
+                    if g == 0:
+                        nc.sync.dma_start(out=w_sb[:], in_=W_k.rearrange("(h p) k -> p h k", p=P))
+            else:
+                nc.sync.dma_start(out=x_v[:], in_=x_units[v])
             x_sb.append(x_v)
             if v == 0:
                 nc.sync.dma_start(out=a2_sb[:], in_=a2)
             if v < QUARTERS:
                 tiles_q = slice(TILES_Q * v, TILES_Q * (v + 1))
                 nc.sync.dma_start(out=a_sb[:, tiles_q, :], in_=a_rows[:, tiles_q, :])
-        ka_b = keep.tile([P, CO], BF16)
-        nc.scalar.dma_start(out=ka_b[:], in_=k_a.rearrange("a b c -> (a b c)").partition_broadcast(P))
-        kk_b = keep.tile([P, CO], BF16)
-        nc.scalar.dma_start(out=kk_b[:], in_=k_k.rearrange("a b c -> (a b c)").partition_broadcast(P))
+        table_in = keep.tile([P, 1], F32)
+        nc.gpsimd.memset(table_in[:], 0.0)
+        table_out = keep.tile([P, 1], F32)
+        nc.scalar.activation(out=table_out[:], in_=table_in[:], func=ACT.Sigmoid)
 
         ident = keep.tile([P, P], BF16)
         make_identity(nc, ident[:])
@@ -100,29 +109,45 @@ def tile_full_tmix_params_pa_t_kernel(tc, x, x_k, W_k, a_hid, a2, a0, k_k, k_a, 
         )
         stay = keep.tile([P, CHUNKS], F32)
         nc.vector.tensor_scalar(out=stay[:], in0=mix[:], scalar1=-1.0, scalar2=1.0, op0=ALU.mult, op1=ALU.add)
+        spread_ps = psum_acc.tile([P, 2, CO], F32, tag="acc")
+        for e, r in enumerate((KK_ROW, KA_ROW)):
+            nc.tensor.matmul(
+                out=spread_ps[:, e, :],
+                lhsT=ident[:, r : r + 1].to_broadcast([P, P]),
+                rhs=rows[:, 0:CO],
+                start=True,
+                stop=True,
+            )
+        spread = keep.tile([P, 2, CO], BF16)
+        nc.scalar.copy(out=spread[:], in_=spread_ps[:])
+        kk_b = spread[:, 0, :]
+        ka_b = spread[:, 1, :]
         a0_cols = keep.tile([P, CO_HALVES, P], F32)
         for h in range(CO_HALVES):
             nc.vector.tensor_copy(
-                out=a0_cols[:, h, :], in_=rows_ps[:, PACK + h, PASSES : PASSES + 1].to_broadcast([P, P])
+                out=a0_cols[:, h, :], in_=rows_ps[:, PACK + h, A0_ROW : A0_ROW + 1].to_broadcast([P, P])
             )
 
         w_codes = keep.tile([P, PASSES, CO], U32, align_bytes=64)
         w_scales = keep.tile([P, PASSES, CO], U8, align_bytes=64)
         for g in range(PASSES):
-            wT_ps = psum_acc.tile([P, PACK, CO], BF16, tag="acc")
-            for j in range(PACK):
+            wT_ps = psum_acc.tile([P, DUOS, CO], F32, tag="acc")
+            for d in range(DUOS):
                 for h in range(CO_HALVES):
                     nc.tensor.transpose(
-                        out=wT_ps[:, j, h * P : (h + 1) * P],
-                        in_=w_sb[:, h, g * P * PACK + j : (g + 1) * P * PACK : PACK],
-                        identity=ident[:],
+                        out=wT_ps[:, d, h * P : (h + 1) * P],
+                        in_=w_sb[:, h, :].bitcast(F32)[:, g * P * DUOS + d : (g + 1) * P * DUOS : DUOS],
+                        identity=ident_f32[:],
                     )
-            w_grouped = work.tile([P, CO, PACK], BF16, align_bytes=64)
-            nc.vector.tensor_copy(out=w_grouped[:], in_=wT_ps[:].rearrange("p j c -> p c j"))
+            w_grouped = work.tile([P, CO * PACK], BF16, align_bytes=64)
+            nc.vector.tensor_copy(
+                out=w_grouped[:].bitcast(F32).rearrange("p (c d) -> p c d", d=DUOS),
+                in_=wT_ps[:].rearrange("p d c -> p c d"),
+            )
             nc.vector.quantize_mx(
                 out=w_codes[:, g, :].bitcast(FP8X4),
                 scales=w_scales[:, g, :],
-                in_=w_grouped[:].rearrange("p c j -> p (c j)"),
+                in_=w_grouped[:],
             )
 
         ahT = keep.tile([P, TILES, P], BF16)
@@ -153,7 +178,7 @@ def tile_full_tmix_params_pa_t_kernel(tc, x, x_k, W_k, a_hid, a2, a0, k_k, k_a, 
                 out=gate1[:, 2 * pair : 2 * pair + 2, :],
                 in0=a_gate[:],
                 scalar=1.0,
-                in1=ka_b[:].unsqueeze(1).to_broadcast([P, 2, CO]),
+                in1=ka_b.unsqueeze(1).to_broadcast([P, 2, CO]),
                 op0=ALU.subtract,
                 op1=ALU.mult,
             )
@@ -175,16 +200,15 @@ def tile_full_tmix_params_pa_t_kernel(tc, x, x_k, W_k, a_hid, a2, a0, k_k, k_a, 
 
         def transpose_x(s):
             v, pos = divmod(s, STEPS_U)
-            bank = psum_t.tile([P, 2, UNIT], BF16, tag="t")
-            for cc in range(2):
-                g, j = divmod(2 * pos + cc, PACK)
-                for n in range(TILES_U):
-                    nc.tensor.transpose(
-                        out=bank[:, cc, n * P : (n + 1) * P],
-                        in_=x_sb[v][:, n, g * P * PACK + j : (g + 1) * P * PACK : PACK],
-                        identity=ident[:],
-                    )
-            xT[s] = bank
+            g, d = divmod(pos, DUOS)
+            bank = psum_t.tile([P, UNIT], F32, tag="t")
+            for n in range(TILES_U):
+                nc.tensor.transpose(
+                    out=bank[:, n * P : (n + 1) * P],
+                    in_=x_sb[v][:, n, :].bitcast(F32)[:, g * P * DUOS + d : (g + 1) * P * DUOS : DUOS],
+                    identity=ident_f32[:],
+                )
+            xT[s] = bank[:].bitcast(BF16).rearrange("p (r c) -> p c r", c=2)
 
         def scale_prev(s):
             v, pos = divmod(s, STEPS_U)
@@ -269,7 +293,7 @@ def tile_full_tmix_params_pa_t_kernel(tc, x, x_k, W_k, a_hid, a2, a0, k_k, k_a, 
             nc.vector.tensor_tensor(
                 out=new_kkh[:].rearrange("p (e h) d -> p e (h d)", e=2),
                 in0=k_ps[pair][:],
-                in1=kk_b[:].unsqueeze(1).to_broadcast([P, 2, CO]),
+                in1=kk_b.unsqueeze(1).to_broadcast([P, 2, CO]),
                 op=ALU.mult,
             )
             kkh[pair] = new_kkh

@@ -118,10 +118,9 @@ def tile_full_tmix_params_pa_t_kernel(tc, x, x_k, W_k, a_hid, a2, a0, k_k, k_a, 
                 start=True,
                 stop=True,
             )
-        spread = keep.tile([P, 2, CO], BF16)
-        nc.scalar.copy(out=spread[:], in_=spread_ps[:])
-        kk_b = spread[:, 0, :]
-        ka_b = spread[:, 1, :]
+        kk_b = keep.tile([P, CO], BF16)
+        nc.scalar.copy(out=kk_b[:], in_=spread_ps[:, 0, :])
+        ka_b = spread_ps[:, 1, :]
         a0_cols = keep.tile([P, CO_HALVES, P], F32)
         for h in range(CO_HALVES):
             nc.vector.tensor_copy(
@@ -293,7 +292,7 @@ def tile_full_tmix_params_pa_t_kernel(tc, x, x_k, W_k, a_hid, a2, a0, k_k, k_a, 
             nc.vector.tensor_tensor(
                 out=new_kkh[:].rearrange("p (e h) d -> p e (h d)", e=2),
                 in0=k_ps[pair][:],
-                in1=kk_b.unsqueeze(1).to_broadcast([P, 2, CO]),
+                in1=kk_b[:].unsqueeze(1).to_broadcast([P, 2, CO]),
                 op=ALU.mult,
             )
             kkh[pair] = new_kkh

@@ -32,6 +32,9 @@ PAIRS_U = TILES_U // 2
 HEADS2 = 2 * CO // HS
 TILES_Q = 8
 QUARTERS = TILES // TILES_Q
+GATES_ROUND = 2
+ROUNDS_QUARTER = TILES_Q // 2 // GATES_ROUND
+ROUNDS_GATE = PAIRS // GATES_ROUND
 EPS_NORM = 1e-12
 
 FLOPS = 2 * B * T * C * CO + 2 * B * T * DA * CO
@@ -49,6 +52,7 @@ def tile_full_tmix_params_pa_t_kernel(tc, x, x_k, W_k, a_hid, a2, a0, k_k, k_a, 
         work = ctx.enter_context(tc.tile_pool(name="work", bufs=2))
         mx = ctx.enter_context(tc.tile_pool(name="mx", bufs=4))
         tail = ctx.enter_context(tc.tile_pool(name="tail", bufs=3))
+        norms = ctx.enter_context(tc.tile_pool(name="norms", bufs=8))
         psum_t = ctx.enter_context(tc.psum_pool(name="psum_t", bufs=4))
         psum_acc = ctx.enter_context(tc.psum_pool(name="psum_acc", bufs=4))
 
@@ -158,7 +162,7 @@ def tile_full_tmix_params_pa_t_kernel(tc, x, x_k, W_k, a_hid, a2, a0, k_k, k_a, 
                 nc.tensor.transpose(out=ahT_ps[:, n, :], in_=a_sb[:, TILES_Q * q + n, :], identity=ident[:])
             nc.scalar.copy(out=ahT[:, TILES_Q * q : TILES_Q * (q + 1), :], in_=ahT_ps[:])
 
-        def gate(pair):
+        def sigmoids(pair):
             z_ps = psum_acc.tile([P, 2, CO], F32, tag="acc")
             for e in range(2):
                 for h in range(CO_HALVES):
@@ -171,20 +175,18 @@ def tile_full_tmix_params_pa_t_kernel(tc, x, x_k, W_k, a_hid, a2, a0, k_k, k_a, 
                         stop=False,
                     )
                 nc.tensor.matmul(out=z_ps[:, e, :], lhsT=ahT[:, 2 * pair + e, :], rhs=a2_sb[:], start=False, stop=True)
-            a_gate = tail.tile([P, 2, CO], F32)
-            nc.scalar.activation(out=a_gate[:], in_=z_ps[:], func=ACT.Sigmoid)
+            nc.scalar.activation(out=gate1[:, 2 * pair : 2 * pair + 2, :], in_=z_ps[:], func=ACT.Sigmoid)
+
+        def gate(i):
+            tiles = slice(2 * GATES_ROUND * i, 2 * GATES_ROUND * (i + 1))
             nc.vector.scalar_tensor_tensor(
-                out=gate1[:, 2 * pair : 2 * pair + 2, :],
-                in0=a_gate[:],
+                out=gate1[:, tiles, :],
+                in0=gate1[:, tiles, :],
                 scalar=1.0,
-                in1=ka_b.unsqueeze(1).to_broadcast([P, 2, CO]),
+                in1=ka_b.unsqueeze(1).to_broadcast([P, 2 * GATES_ROUND, CO]),
                 op0=ALU.subtract,
                 op1=ALU.mult,
             )
-
-        def gate_quarter(q):
-            for pair in range(TILES_Q // 2 * q, TILES_Q // 2 * (q + 1)):
-                gate(pair)
 
         xT = {}
         planes = {}
@@ -288,7 +290,7 @@ def tile_full_tmix_params_pa_t_kernel(tc, x, x_k, W_k, a_hid, a2, a0, k_k, k_a, 
             k_ps[pair] = acc
 
         def scale_k(pair):
-            new_kkh = tail.tile([P, HEADS2, HS], F32, tag="kkh")
+            new_kkh = norms.tile([P, HEADS2, HS], F32, tag="kkh")
             nc.vector.tensor_tensor(
                 out=new_kkh[:].rearrange("p (e h) d -> p e (h d)", e=2),
                 in0=k_ps[pair][:],
@@ -296,6 +298,8 @@ def tile_full_tmix_params_pa_t_kernel(tc, x, x_k, W_k, a_hid, a2, a0, k_k, k_a, 
                 op=ALU.mult,
             )
             kkh[pair] = new_kkh
+
+        def gate_k(pair):
             k_out_sb = tail.tile([P, 2, CO], F32)
             nc.vector.scalar_tensor_tensor(
                 out=k_out_sb[:],
@@ -309,7 +313,7 @@ def tile_full_tmix_params_pa_t_kernel(tc, x, x_k, W_k, a_hid, a2, a0, k_k, k_a, 
 
         def sum_squares(pair):
             squares = tail.tile([P, HEADS2, HS], F32)
-            new_sumsq = tail.tile([P, HEADS2], F32, tag="sumsq")
+            new_sumsq = norms.tile([P, HEADS2], F32, tag="sumsq")
             for h in range(HEADS2):
                 nc.scalar.activation(
                     out=squares[:, h, :], in_=kkh[pair][:, h, :], func=ACT.Square, accum_out=new_sumsq[:, h : h + 1]
@@ -317,12 +321,12 @@ def tile_full_tmix_params_pa_t_kernel(tc, x, x_k, W_k, a_hid, a2, a0, k_k, k_a, 
             sumsq[pair] = new_sumsq
 
         def floor_sum(pair):
-            new_floored = tail.tile([P, HEADS2], F32, tag="floored")
+            new_floored = norms.tile([P, HEADS2], F32, tag="floored")
             nc.scalar.activation(out=new_floored[:], in_=sumsq[pair][:], func=ACT.Relu, bias=neg_eps2[:])
             floored[pair] = new_floored
 
         def invert_norm(pair):
-            new_inv = tail.tile([P, HEADS2], F32, tag="inv_norm")
+            new_inv = norms.tile([P, HEADS2], F32, tag="inv_norm")
             nc.scalar.activation(out=new_inv[:], in_=floored[pair][:], func=ACT.Abs_reciprocal_sqrt, bias=eps2[:])
             inv_norm[pair] = new_inv
 
@@ -336,6 +340,8 @@ def tile_full_tmix_params_pa_t_kernel(tc, x, x_k, W_k, a_hid, a2, a0, k_k, k_a, 
                 out=kk_v[:, 2 * pair : 2 * pair + 2, :], in_=kk_sb[:].rearrange("p (e h) d -> p e (h d)", e=2)
             )
 
+        invert_round = [max(pair + 4, ROUNDS_GATE) for pair in range(PAIRS)]
+        divide_round = [max(pair + 5, ROUNDS_GATE + 1 + pair // 2) for pair in range(PAIRS)]
         for s in range(3):
             transpose_x(s)
         for s in range(2):
@@ -345,12 +351,14 @@ def tile_full_tmix_params_pa_t_kernel(tc, x, x_k, W_k, a_hid, a2, a0, k_k, k_a, 
             if 0 <= i - 4 < PAIRS:
                 sum_squares(i - 4)
             step(2 * i)
-            if 0 <= i - 4 < PAIRS:
-                floor_sum(i - 4)
-            if 0 <= i - 5 < PAIRS:
-                divide(i - 5)
-            if 0 <= i - 4 < PAIRS:
-                invert_norm(i - 4)
+            inverted = [pair for pair in range(PAIRS) if invert_round[pair] == i]
+            for pair in inverted:
+                floor_sum(pair)
+            for pair in range(PAIRS):
+                if divide_round[pair] == i:
+                    divide(pair)
+            for pair in inverted:
+                invert_norm(pair)
             step(2 * i + 1)
             if 0 <= i - 1 < GROUPS:
                 quantise(i - 1)
@@ -358,9 +366,17 @@ def tile_full_tmix_params_pa_t_kernel(tc, x, x_k, W_k, a_hid, a2, a0, k_k, k_a, 
                 regroup(i)
             if 0 <= i - 3 < PAIRS:
                 scale_k(i - 3)
-            if i < QUARTERS:
-                gate_quarter(i)
-            if i + 1 < QUARTERS:
-                transpose_a_hid(i + 1)
+            if 0 <= i - 3 < PAIRS - PAIRS_U:
+                gate_k(i - 3)
+            if i - 3 == PAIRS - 1:
+                for pair in range(PAIRS - PAIRS_U, PAIRS):
+                    gate_k(pair)
+            if i < ROUNDS_GATE:
+                for pair in range(GATES_ROUND * i, GATES_ROUND * (i + 1)):
+                    sigmoids(pair)
+                gate(i)
+            q, rest = divmod(i + 1, ROUNDS_QUARTER)
+            if rest == 0 and q < QUARTERS:
+                transpose_a_hid(q)
             if 0 <= i - 2 < PAIRS:
                 project(i - 2)

from contextlib import ExitStack

import concourse.mybir as mybir
from concourse.masks import make_identity

F32 = mybir.dt.float32
BF16 = mybir.dt.bfloat16
U32 = mybir.dt.uint32
U8 = mybir.dt.uint8
FP8X4 = mybir.dt.float8_e4m3fn_x4
ALU = mybir.AluOpType
ACT = mybir.ActivationFunctionType

P = 128
PACK = 4
B, T, C, CO, HS, DA = 4, 1024, 1024, 256, 64, 128
PASSES = C // (P * PACK)
CHUNKS = C // P
CO_HALVES = CO // P
DUOS = PACK // 2
A0_ROW, KK_ROW, KA_ROW = PASSES, PASSES + 1, PASSES + 2
UNIT = 512
UNITS = B * T // UNIT
UNITS_T = T // UNIT
TILES_U = UNIT // P
TILES = B * T // P
STEPS_U = CHUNKS // 2
STEPS = UNITS * STEPS_U
GROUPS = UNITS * PASSES
PAIRS = TILES // 2
PAIRS_U = TILES_U // 2
HEADS2 = 2 * CO // HS
TILES_Q = 8
QUARTERS = TILES // TILES_Q
GATES_ROUND = 2
ROUNDS_QUARTER = TILES_Q // 2 // GATES_ROUND
ROUNDS_GATE = PAIRS // GATES_ROUND
EPS_NORM = 1e-12

FLOPS = 2 * B * T * C * CO + 2 * B * T * DA * CO


def tile_full_tmix_params_pa_t_kernel(tc, x, x_k, W_k, a_hid, a2, a0, k_k, k_a, out_0, out_1):
    nc = tc.nc
    x_units = x.flatten_outer_dims().rearrange("(v n p) k -> v p n k", n=TILES_U, p=P)
    a_rows = a_hid.flatten_outer_dims().rearrange("(n p) k -> p n k", p=P)
    k_out_v = out_0.flatten_outer_dims().rearrange("(n p) c -> p n c", p=P)
    kk_v = out_1.flatten_outer_dims().rearrange("(n p) c -> p n c", p=P)

    with ExitStack() as ctx:
        keep = ctx.enter_context(tc.tile_pool(name="keep", bufs=1))
        work = ctx.enter_context(tc.tile_pool(name="work", bufs=2))
        mx = ctx.enter_context(tc.tile_pool(name="mx", bufs=4))
        tail = ctx.enter_context(tc.tile_pool(name="tail", bufs=3))
        norms = ctx.enter_context(tc.tile_pool(name="norms", bufs=8))
        psum_t = ctx.enter_context(tc.psum_pool(name="psum_t", bufs=4))
        psum_acc = ctx.enter_context(tc.psum_pool(name="psum_acc", bufs=4))

        rows = keep.tile([P, P * PACK], BF16)
        nc.gpsimd.memset(rows[:], 0.0)
        nc.sync.dma_start(out=rows[0:PASSES, :], in_=x_k.rearrange("a b (g c) -> (a b g) c", g=PASSES))
        for r, vector in ((A0_ROW, a0), (KK_ROW, k_k), (KA_ROW, k_a)):
            nc.sync.dma_start(out=rows[r : r + 1, 0:CO], in_=vector.rearrange("a b c -> (a b) c"))
        w_sb = keep.tile([P, CO_HALVES, C], BF16)
        a2_sb = keep.tile([P, CO], BF16)
        a_sb = keep.tile([P, TILES, DA], BF16)
        x_sb = []
        for v in range(UNITS):
            x_v = keep.tile([P, TILES_U, C], BF16, name="x_sb%d" % v)
            if v == 0:
                for g in range(PASSES):
                    channels = slice(g * P * PACK, (g + 1) * P * PACK)
                    nc.sync.dma_start(out=x_v[:, :, channels], in_=x_units[v][:, :, channels])
                    if g == 0:
                        nc.sync.dma_start(out=w_sb[:], in_=W_k.rearrange("(h p) k -> p h k", p=P))
            else:
                nc.sync.dma_start(out=x_v[:], in_=x_units[v])
            x_sb.append(x_v)
            if v == 0:
                nc.sync.dma_start(out=a2_sb[:], in_=a2)
            if v < QUARTERS:
                tiles_q = slice(TILES_Q * v, TILES_Q * (v + 1))
                nc.sync.dma_start(out=a_sb[:, tiles_q, :], in_=a_rows[:, tiles_q, :])
        table_in = keep.tile([P, 1], F32)
        nc.gpsimd.memset(table_in[:], 0.0)
        table_out = keep.tile([P, 1], F32)
        nc.scalar.activation(out=table_out[:], in_=table_in[:], func=ACT.Sigmoid)

        ident = keep.tile([P, P], BF16)
        make_identity(nc, ident[:])
        ident_f32 = keep.tile([P, P], F32)
        make_identity(nc, ident_f32[:])

        u = []
        for chunk in range(CHUNKS):
            u_c = keep.tile([P, T + 1], F32, name="u%d" % chunk)
            nc.vector.memset(u_c[:, 0:1], 0.0)
            u.append(u_c)
        eps2 = keep.tile([P, 1], F32)
        nc.vector.memset(eps2[:], EPS_NORM * EPS_NORM)
        neg_eps2 = keep.tile([P, 1], F32)
        nc.vector.memset(neg_eps2[:], -EPS_NORM * EPS_NORM)

        rows_ps = psum_t.tile([P, PACK + CO_HALVES, P], BF16, tag="t")
        for j in range(PACK):
            nc.tensor.transpose(out=rows_ps[:, j, :], in_=rows[:, j : P * PACK : PACK], identity=ident[:])
        for h in range(CO_HALVES):
            nc.tensor.transpose(out=rows_ps[:, PACK + h, :], in_=rows[:, h * P : (h + 1) * P], identity=ident[:])
        mix = keep.tile([P, CHUNKS], F32)
        nc.vector.tensor_copy(
            out=mix[:].rearrange("p (g j) -> p g j", g=PASSES),
            in_=rows_ps[:, 0:PACK, 0:PASSES].rearrange("p j g -> p g j"),
        )
        stay = keep.tile([P, CHUNKS], F32)
        nc.vector.tensor_scalar(out=stay[:], in0=mix[:], scalar1=-1.0, scalar2=1.0, op0=ALU.mult, op1=ALU.add)
        spread_ps = psum_acc.tile([P, 2, CO], F32, tag="acc")
        for e, r in enumerate((KK_ROW, KA_ROW)):
            nc.tensor.matmul(
                out=spread_ps[:, e, :],
                lhsT=ident[:, r : r + 1].to_broadcast([P, P]),
                rhs=rows[:, 0:CO],
                start=True,
                stop=True,
            )
        kk_b = keep.tile([P, CO], BF16)
        nc.scalar.copy(out=kk_b[:], in_=spread_ps[:, 0, :])
        ka_b = spread_ps[:, 1, :]
        a0_cols = keep.tile([P, CO_HALVES, P], F32)
        for h in range(CO_HALVES):
            nc.vector.tensor_copy(
                out=a0_cols[:, h, :], in_=rows_ps[:, PACK + h, A0_ROW : A0_ROW + 1].to_broadcast([P, P])
            )

        w_codes = keep.tile([P, PASSES, CO], U32, align_bytes=64)
        w_scales = keep.tile([P, PASSES, CO], U8, align_bytes=64)
        for g in range(PASSES):
            wT_ps = psum_acc.tile([P, DUOS, CO], F32, tag="acc")
            for d in range(DUOS):
                for h in range(CO_HALVES):
                    nc.tensor.transpose(
                        out=wT_ps[:, d, h * P : (h + 1) * P],
                        in_=w_sb[:, h, :].bitcast(F32)[:, g * P * DUOS + d : (g + 1) * P * DUOS : DUOS],
                        identity=ident_f32[:],
                    )
            w_grouped = work.tile([P, CO * PACK], BF16, align_bytes=64)
            nc.vector.tensor_copy(
                out=w_grouped[:].bitcast(F32).rearrange("p (c d) -> p c d", d=DUOS),
                in_=wT_ps[:].rearrange("p d c -> p c d"),
            )
            nc.vector.quantize_mx(
                out=w_codes[:, g, :].bitcast(FP8X4),
                scales=w_scales[:, g, :],
                in_=w_grouped[:],
            )

        ahT = keep.tile([P, TILES, P], BF16)
        gate1 = keep.tile([P, TILES, CO], F32)

        def transpose_a_hid(q):
            ahT_ps = psum_acc.tile([P, TILES_Q, P], BF16, tag="acc")
            for n in range(TILES_Q):
                nc.tensor.transpose(out=ahT_ps[:, n, :], in_=a_sb[:, TILES_Q * q + n, :], identity=ident[:])
            nc.scalar.copy(out=ahT[:, TILES_Q * q : TILES_Q * (q + 1), :], in_=ahT_ps[:])

        def sigmoids(pair):
            z_ps = psum_acc.tile([P, 2, CO], F32, tag="acc")
            for e in range(2):
                for h in range(CO_HALVES):
                    nc.tensor.matmul(
                        out=z_ps[:, e, h * P : (h + 1) * P],
                        lhsT=a0_cols[:, h, :],
                        rhs=ident_f32[:],
                        is_transpose=True,
                        start=(h == 0),
                        stop=False,
                    )
                nc.tensor.matmul(out=z_ps[:, e, :], lhsT=ahT[:, 2 * pair + e, :], rhs=a2_sb[:], start=False, stop=True)
            nc.scalar.activation(out=gate1[:, 2 * pair : 2 * pair + 2, :], in_=z_ps[:], func=ACT.Sigmoid)

        def gate(i):
            tiles = slice(2 * GATES_ROUND * i, 2 * GATES_ROUND * (i + 1))
            nc.vector.scalar_tensor_tensor(
                out=gate1[:, tiles, :],
                in0=gate1[:, tiles, :],
                scalar=1.0,
                in1=ka_b.unsqueeze(1).to_broadcast([P, 2 * GATES_ROUND, CO]),
                op0=ALU.subtract,
                op1=ALU.mult,
            )

        xT = {}
        planes = {}
        grouped = {}
        codes = {}
        scales = {}
        k_ps = {}
        kkh = {}
        sumsq = {}
        floored = {}
        inv_norm = {}

        def transpose_x(s):
            v, pos = divmod(s, STEPS_U)
            g, d = divmod(pos, DUOS)
            bank = psum_t.tile([P, UNIT], F32, tag="t")
            for n in range(TILES_U):
                nc.tensor.transpose(
                    out=bank[:, n * P : (n + 1) * P],
                    in_=x_sb[v][:, n, :].bitcast(F32)[:, g * P * DUOS + d : (g + 1) * P * DUOS : DUOS],
                    identity=ident_f32[:],
                )
            xT[s] = bank[:].bitcast(BF16).rearrange("p (r c) -> p c r", c=2)

        def scale_prev(s):
            v, pos = divmod(s, STEPS_U)
            first = UNIT * (v % UNITS_T)
            for cc in range(2):
                chunk = 2 * pos + cc
                nc.scalar.activation(
                    out=u[chunk][:, first + 1 : first + 1 + UNIT],
                    in_=xT[s][:, cc, :],
                    func=ACT.Copy,
                    scale=mix[:, chunk : chunk + 1],
                )

        def mix_tokens(s):
            v, pos = divmod(s, STEPS_U)
            first = UNIT * (v % UNITS_T)
            i = s // 2
            if s % 2 == 0:
                new_planes = work.tile([P, PACK, UNIT], BF16, tag="planes")
                planes[i] = new_planes
            for cc in range(2):
                chunk = 2 * pos + cc
                nc.vector.scalar_tensor_tensor(
                    out=planes[i][:, chunk % PACK, :],
                    in0=xT[s][:, cc, :],
                    scalar=stay[:, chunk : chunk + 1],
                    in1=u[chunk][:, first : first + UNIT],
                    op0=ALU.mult,
                    op1=ALU.add,
                )

        def step(s):
            if s + 3 < STEPS:
                transpose_x(s + 3)
            if s + 2 < STEPS:
                scale_prev(s + 2)
            if s < STEPS:
                mix_tokens(s)

        def regroup(i):
            new_grouped = keep.tile([P, UNIT, PACK], BF16, align_bytes=64, tag="grouped")
            nc.gpsimd.tensor_scalar(
                out=new_grouped[:],
                in0=planes[i][:].rearrange("p j r -> p r j"),
                scalar1=1.0,
                scalar2=0.0,
                op0=ALU.mult,
                op1=ALU.add,
            )
            grouped[i] = new_grouped

        def quantise(i):
            new_codes = mx.tile([P, UNIT], U32, align_bytes=64, tag="codes")
            new_scales = mx.tile([P, UNIT], U8, align_bytes=64, tag="scales")
            nc.vector.quantize_mx(
                out=new_codes[:].bitcast(FP8X4),
                scales=new_scales[:],
                in_=grouped[i][:].rearrange("p r j -> p (r j)"),
            )
            codes[i] = new_codes
            scales[i] = new_scales

        def project(pair):
            v, pos = divmod(pair, PAIRS_U)
            acc = psum_acc.tile([P, 2, CO], F32, tag="acc")
            for e in range(2):
                tokens = slice((2 * pos + e) * P, (2 * pos + e + 1) * P)
                for g in range(PASSES):
                    nc.tensor.matmul_mx(
                        out=acc[:, e, :],
                        lhsT=codes[PASSES * v + g][:, tokens].bitcast(FP8X4),
                        lhsT_scale=scales[PASSES * v + g][:, tokens],
                        rhs=w_codes[:, g, :].bitcast(FP8X4),
                        rhs_scale=w_scales[:, g, :],
                        start=(g == 0),
                        stop=(g == PASSES - 1),
                    )
            k_ps[pair] = acc

        def scale_k(pair):
            new_kkh = norms.tile([P, HEADS2, HS], F32, tag="kkh")
            nc.vector.tensor_tensor(
                out=new_kkh[:].rearrange("p (e h) d -> p e (h d)", e=2),
                in0=k_ps[pair][:],
                in1=kk_b[:].unsqueeze(1).to_broadcast([P, 2, CO]),
                op=ALU.mult,
            )
            kkh[pair] = new_kkh

        def gate_k(pair):
            k_out_sb = tail.tile([P, 2, CO], F32)
            nc.vector.scalar_tensor_tensor(
                out=k_out_sb[:],
                in0=gate1[:, 2 * pair : 2 * pair + 2, :],
                scalar=1.0,
                in1=k_ps[pair][:],
                op0=ALU.add,
                op1=ALU.mult,
            )
            nc.sync.dma_start(out=k_out_v[:, 2 * pair : 2 * pair + 2, :], in_=k_out_sb[:])

        def sum_squares(pair):
            squares = tail.tile([P, HEADS2, HS], F32)
            new_sumsq = norms.tile([P, HEADS2], F32, tag="sumsq")
            for h in range(HEADS2):
                nc.scalar.activation(
                    out=squares[:, h, :], in_=kkh[pair][:, h, :], func=ACT.Square, accum_out=new_sumsq[:, h : h + 1]
                )
            sumsq[pair] = new_sumsq

        def floor_sum(pair):
            new_floored = norms.tile([P, HEADS2], F32, tag="floored")
            nc.scalar.activation(out=new_floored[:], in_=sumsq[pair][:], func=ACT.Relu, bias=neg_eps2[:])
            floored[pair] = new_floored

        def invert_norm(pair):
            new_inv = norms.tile([P, HEADS2], F32, tag="inv_norm")
            nc.scalar.activation(out=new_inv[:], in_=floored[pair][:], func=ACT.Abs_reciprocal_sqrt, bias=eps2[:])
            inv_norm[pair] = new_inv

        def divide(pair):
            kk_sb = tail.tile([P, HEADS2, HS], F32)
            for h in range(HEADS2):
                nc.scalar.activation(
                    out=kk_sb[:, h, :], in_=kkh[pair][:, h, :], func=ACT.Copy, scale=inv_norm[pair][:, h : h + 1]
                )
            nc.sync.dma_start(
                out=kk_v[:, 2 * pair : 2 * pair + 2, :], in_=kk_sb[:].rearrange("p (e h) d -> p e (h d)", e=2)
            )

        invert_round = [max(pair + 4, ROUNDS_GATE) for pair in range(PAIRS)]
        divide_round = [max(pair + 5, ROUNDS_GATE + 1 + pair // 2) for pair in range(PAIRS)]
        for s in range(3):
            transpose_x(s)
        for s in range(2):
            scale_prev(s)
        transpose_a_hid(0)
        for i in range(GROUPS + 5):
            if 0 <= i - 4 < PAIRS:
                sum_squares(i - 4)
            step(2 * i)
            inverted = [pair for pair in range(PAIRS) if invert_round[pair] == i]
            for pair in inverted:
                floor_sum(pair)
            for pair in range(PAIRS):
                if divide_round[pair] == i:
                    divide(pair)
            for pair in inverted:
                invert_norm(pair)
            step(2 * i + 1)
            if 0 <= i - 1 < GROUPS:
                quantise(i - 1)
            if i < GROUPS:
                regroup(i)
            if 0 <= i - 3 < PAIRS:
                scale_k(i - 3)
            if 0 <= i - 3 < PAIRS - PAIRS_U:
                gate_k(i - 3)
            if i - 3 == PAIRS - 1:
                for pair in range(PAIRS - PAIRS_U, PAIRS):
                    gate_k(pair)
            if i < ROUNDS_GATE:
                for pair in range(GATES_ROUND * i, GATES_ROUND * (i + 1)):
                    sigmoids(pair)
                gate(i)
            q, rest = divmod(i + 1, ROUNDS_QUARTER)
            if rest == 0 and q < QUARTERS:
                transpose_a_hid(q)
            if 0 <= i - 2 < PAIRS:
                project(i - 2)
